import numpy as np
import ml_dtypes


def mxq(x, axis, fmt="e4m3"):
    dtype, down = {"e4m3": (ml_dtypes.float8_e4m3fn, 7), "e5m2": (ml_dtypes.float8_e5m2, 14)}[fmt]
    v = np.moveaxis(np.asarray(x, np.float32).astype(ml_dtypes.bfloat16).astype(np.float64), axis, -1)
    blocks = v.reshape(v.shape[:-1] + (-1, 32))
    amax = np.abs(blocks).max(-1, keepdims=True)
    byte = np.maximum(np.where(amax > 0, np.frexp(amax)[1] - 1 + 127, 0) - down, 1)
    scale = np.exp2(byte - 127.0)
    codes = (blocks / scale).astype(np.float32).astype(dtype).astype(np.float64)
    return np.moveaxis((codes * scale).reshape(v.shape), -1, axis)


WIDE = False


def mx_kscale(k):
    if not WIDE:
        return np.ones(k)
    levels = np.array([10, -10, 5, -5, 0])
    if k % 512:
        return np.exp2(np.random.permutation(np.resize(levels, k // 32))).repeat(32)
    a = np.empty((k // 512, 16))
    for p in range(k // 512):
        a[p, :8] = np.random.permutation(np.resize(levels, 8))
        for g in range(8):
            far = levels[np.abs(levels - a[p, g]) >= 10]
            a[p, g + 8] = far[np.random.randint(len(far))]
    return np.exp2(a.ravel()).repeat(32)


BF16 = ml_dtypes.bfloat16


def bf(x):
    return np.asarray(x, np.float32).astype(BF16)


def f64(x):
    return np.asarray(x).astype(np.float64)


M, SP, H, FF, NH = 2560, 1920, 2048, 5120, 16
EPS = 1.1920929e-07


def rms_norm(x, w):
    var = np.mean(np.square(x), axis=-1, keepdims=True)
    return x * (1.0 / np.sqrt(var + EPS)) * w


def silu(v):
    return v / (1.0 + np.exp(-v))


def setup_inputs():
    s, t = mx_kscale(H), mx_kscale(H)
    return {"attn": bf(np.random.standard_normal((M, H)) * 0.25 * s),
            "x": bf(np.random.standard_normal((M, H))),
            "W_o": bf(np.random.standard_normal((2, H, H)) * 2.0 / np.sqrt(H) / s[None, :, None]),
            "W_gu": bf(np.random.standard_normal((2, H, 2 * FF)) / np.sqrt(H) / t[None, :, None]),
            "ln2": bf((1.0 + 0.1 * np.random.standard_normal((2, H))) * t)}


def reference(attn, x, W_o, W_gu, ln2):
    attn, x, W_o, W_gu, ln2 = f64(attn), f64(x), f64(W_o), f64(W_gu), f64(ln2)
    o0 = mxq(attn[:SP], 1, "e4m3") @ mxq(W_o[0], 0, "e4m3")
    o1 = mxq(attn[SP:], 1, "e4m3") @ mxq(W_o[1], 0, "e4m3")
    x_mid = x + np.concatenate([o0, o1], axis=0)
    h0 = rms_norm(x_mid[:SP], ln2[0])
    h1 = rms_norm(x_mid[SP:], ln2[1])
    gu0 = mxq(h0, 1, "e4m3") @ mxq(W_gu[0], 0, "e4m3")
    gu1 = mxq(h1, 1, "e4m3") @ mxq(W_gu[1], 0, "e4m3")
    gu = np.concatenate([gu0, gu1], axis=0)
    gate, up = np.split(gu, 2, axis=-1)
    return x_mid, silu(gate) * up

@@ -1,0 +1,385 @@
+from contextlib import ExitStack
+
+import concourse.mybir as mybir
+from concourse.masks import make_identity
+
+F32 = mybir.dt.float32
+BF16 = mybir.dt.bfloat16
+U32 = mybir.dt.uint32
+U8 = mybir.dt.uint8
+FP8X4 = mybir.dt.float8_e4m3fn_x4
+ACT = mybir.ActivationFunctionType
+ALU = mybir.AluOpType
+
+ROWS, ROWS0, H, FF = 2560, 1920, 2048, 5120
+EPS = 1.1920929e-07
+FLOPS = 2 * ROWS * H * (H + 2 * FF)
+
+P = 128
+K_PASS = 4 * P
+KP = H // K_PASS
+NB = 512
+TILES = ROWS // P
+TILES0 = ROWS0 // P
+CHUNKS = FF // NB
+UNITS = 2 * KP
+
+RAW_BUFS = 6
+GRP_BUFS = 4
+JOB_BUFS = 4
+QUANT_LAG = 2
+MANUAL = True
+DRAIN_STEPS = 1
+S1_VEC = 2
+S1_TICKS = ({"a":0,"b":0,"c":0,"d":1}, {"a": 0, "b": 0, "c": 0, "d": 0})
+S1_STEPS = ({"a": 0, "b": 0, "c": 0, "d": 2}, {"a": 1, "b": 1, "c": 1, "d": 1})
+
+
+def tile_twomodelblockrouted_pb_l_kernel(tc, attn, x, W_o, W_gu, ln2, out_0, out_1):
+    nc = tc.nc
+    with ExitStack() as ctx:
+        const = ctx.enter_context(tc.tile_pool(name="const", bufs=1))
+        rawp = ctx.enter_context(tc.tile_pool(name="rawp", bufs=RAW_BUFS))
+        grpp = ctx.enter_context(tc.tile_pool(name="grpp", bufs=GRP_BUFS))
+        wpool = ctx.enter_context(tc.tile_pool(name="wpool", bufs=JOB_BUFS))
+        actp = ctx.enter_context(tc.tile_pool(name="actp", bufs=2))
+        smallp = ctx.enter_context(tc.tile_pool(name="smallp", bufs=3))
+        epi = ctx.enter_context(tc.tile_pool(name="epi", bufs=4))
+        accp = ctx.enter_context(tc.psum_pool(name="accp", bufs=6))
+        trp = ctx.enter_context(tc.psum_pool(name="trp", bufs=2))
+
+        ident = const.tile([P, P], F32, name="ident", tag="ident")
+        make_identity(nc, ident[:])
+        neg_half = const.tile([P, 1], F32, name="neg_half", tag="neg_half")
+        nc.gpsimd.memset(neg_half[:], -0.5)
+        warm = const.tile([P, 1], F32, name="warm", tag="warm")
+        nc.gpsimd.memset(warm[:], 0.0)
+        warm2 = const.tile([P, 1], F32, name="warm2", tag="warm2")
+        nc.scalar.activation(out=warm2[:], in_=warm[:], func=ACT.Silu)
+        junk = const.tile([P, H // 2], BF16, name="junk", tag="junk")
+        ln2b = [const.tile([P, H], BF16, name="ln2b%d" % g, tag="ln2b%d" % g) for g in range(2)]
+        hc = const.tile([P, TILES, KP, P], U32, name="hc", tag="hc", align_bytes=64)
+        hs = const.tile([P, TILES, P], U8, name="hs", tag="hs", align_bytes=64)
+
+        job_list = [("o", 0, 0), ("o", 0, 1), ("g", 0, 0), ("g", 0, 1), ("g", 0, 2), ("g", 0, 3), ("o", 1, 0), ("o", 1, 1), ("g", 0, 4)]
+        c1 = 0
+        for c0 in range(5, CHUNKS):
+            job_list.extend([("g", 1, c1), ("g", 1, c1 + 1), ("g", 0, c0)])
+            c1 += 2
+        jobs = []
+        steps = {}
+        wo_job = {}
+        for j, jb in enumerate(job_list):
+            kind, g, c = jb
+            if kind == "o":
+                jobs.append((W_o[g], (2 * c * NB, (2 * c + 1) * NB)))
+                wo_job[(g, c)] = j
+            else:
+                jobs.append((W_gu[g], (c * NB, FF + c * NB)))
+                steps[j] = [(c, i) for i in (range(TILES0) if g == 0 else range(TILES0, TILES))]
+        finished = [False for jb in jobs]
+
+        st = {"copy": 0, "quant": 0, "load": 0, "lo": 0, "hi": TILES0}
+        h_ready = set()
+        st["who"] = lambda t: t % 2 == 0
+        raws, grps, codes = {}, {}, {}
+        araw, xraw, gat, acod, xm, hsort, sums, rstd = {}, {}, {}, {}, {}, {}, {}, {}
+        n_units = UNITS * len(jobs)
+
+        def unit_load():
+            t = st["load"]
+            if t >= n_units:
+                return
+            w, cols = jobs[t // UNITS]
+            kp, hf = (t % UNITS) // 2, t % 2
+            raw = rawp.tile([P, 4, NB], BF16, name="raw", tag="raw")
+            nc.sync.dma_start(
+                out=raw[:],
+                in_=w[kp * K_PASS : (kp + 1) * K_PASS, cols[hf] : cols[hf] + NB].rearrange("(p j) w -> p j w", j=4),
+            )
+            raws[t] = raw
+            st["load"] = t + 1
+
+        def unit_copy():
+            t = st["copy"]
+            grp = grpp.tile([P, 4 * NB], BF16, name="grp", tag="grp", align_bytes=64)
+            dst = grp[:].rearrange("p (w j) -> p w j", j=4)
+            src = raws[t][:].rearrange("p j w -> p w j")
+            if st["who"](t):
+                nc.vector.tensor_copy(out=dst, in_=src)
+            else:
+                nc.scalar.copy(out=dst, in_=src)
+            grps[t] = grp
+            st["copy"] = t + 1
+
+        def unit_quant():
+            t = st["quant"]
+            j = t // UNITS
+            kp, hf = (t % UNITS) // 2, t % 2
+            if t % UNITS == 0:
+                wc = wpool.tile([P, KP, 2 * NB], U32, name="wc", tag="wc", align_bytes=64)
+                ws = wpool.tile([P, 2 * NB], U8, name="ws", tag="ws", align_bytes=64)
+                codes[j] = (wc, ws)
+            wc, ws = codes[j]
+            nc.vector.quantize_mx(
+                out=wc[:, kp, hf * NB : (hf + 1) * NB].bitcast(FP8X4),
+                scales=ws[4 * kp :, hf * NB : (hf + 1) * NB],
+                in_=grps[t][:],
+            )
+            st["quant"] = t + 1
+
+        def job_free(j):
+            return sum(1 for k in range(j) if not finished[k]) < JOB_BUFS
+
+        def tick(flush):
+            t = st["copy"]
+            copied = False
+            if flush and t >= flush:
+                unit_quant()
+                return
+            if t < n_units and job_free(t // UNITS):
+                unit_copy()
+                unit_load()
+                copied = True
+            lag = QUANT_LAG if copied else 0
+            if st["quant"] < st["copy"] - lag:
+                unit_quant()
+
+        def load_attn(i):
+            if i < st["hi"]:
+                t = actp.tile([P, H], BF16, name="araw", tag="araw")
+                nc.sync.dma_start(out=t[:], in_=attn[i * P : (i + 1) * P, :])
+                araw[i] = t
+
+        def load_x(i):
+            if i < st["hi"]:
+                t = actp.tile([P, H], BF16, name="xraw", tag="xraw")
+                nc.sync.dma_start(out=t[:], in_=x[i * P : (i + 1) * P, :])
+                xraw[i] = t
+
+        def transposes(word_slice):
+            g = actp.tile([P, H], BF16, name="gact", tag="gact", align_bytes=64)
+            gw = g[:].bitcast(F32)
+            for b in range(2):
+                tr = trp.tile([P, NB], F32, name="tr", tag="tr")
+                for a in range(2):
+                    for u in range(2):
+                        nc.tensor.transpose(tr[:, (2 * a + u) * P : (2 * a + u + 1) * P], word_slice(2 * b + a, u), ident[:])
+                nc.scalar.copy(
+                    out=gw[:, NB * b : NB * (b + 1)].rearrange("p (a r u) -> p a r u", a=2, u=2),
+                    in_=tr[:].rearrange("p (a u r) -> p a r u", a=2, u=2),
+                )
+            return g
+
+        def attn_transposes(i):
+            words = araw[i][:].bitcast(F32)
+            gat[i] = transposes(lambda kp, u: words[:, 256 * kp + u : 256 * (kp + 1) : 2])
+            if i > 0:
+                load_attn(i + 2)
+
+        def attn_quant(i):
+            c = actp.tile([P, KP, P], U32, name="ac", tag="ac", align_bytes=64)
+            s = actp.tile([P, KP * P], U8, name="asc", tag="asc", align_bytes=64)
+            nc.vector.quantize_mx(out=c[:].rearrange("p k r -> p (k r)").bitcast(FP8X4), scales=s[:], in_=gat[i][:])
+            acod[i] = (c, s)
+
+        def s1_matmul(i, n):
+            wc, ws = codes[wo_job[(0 if i < TILES0 else 1, n // 2)]]
+            c, s = acod[i]
+            lo = (n % 2) * NB
+            o = accp.tile([P, NB], F32, name="acc", tag="acc")
+            for kp in range(KP):
+                nc.tensor.matmul_mx(
+                    out=o[:],
+                    lhsT=c[:, kp, :].bitcast(FP8X4),
+                    lhsT_scale=s[:, kp * P : (kp + 1) * P],
+                    rhs=wc[:, kp, lo : lo + NB].bitcast(FP8X4),
+                    rhs_scale=ws[4 * kp :, lo : lo + NB],
+                    start=(kp == 0),
+                    stop=(kp == KP - 1),
+                )
+            if n == 0:
+                xm[i] = actp.tile([P, H], F32, name="xm", tag="xm")
+            nc.vector.tensor_tensor(
+                out=xm[i][:, n * NB : (n + 1) * NB], in0=o[:], in1=xraw[i][:, n * NB : (n + 1) * NB], op=ALU.add
+            )
+
+        def square(i, half):
+            if half == 0:
+                sums[i] = smallp.tile([P, 2], F32, name="sums", tag="sums")
+            nc.scalar.activation(
+                out=junk[:],
+                in_=xm[i][:, half * (H // 2) : (half + 1) * (H // 2)],
+                func=ACT.Square,
+                accum_out=sums[i][:, half : half + 1],
+            )
+
+        def inv_rms(i):
+            tot = smallp.tile([P, 1], F32, name="tot", tag="tot")
+            nc.gpsimd.tensor_tensor(out=tot[:], in0=sums[i][:, 0:1], in1=sums[i][:, 1:2], op=ALU.add)
+            var = smallp.tile([P, 1], F32, name="var", tag="var")
+            nc.gpsimd.tensor_scalar(out=var[:], in0=tot[:], scalar1=1.0 / H, scalar2=EPS, op0=ALU.mult, op1=ALU.add)
+            r = smallp.tile([P, 1], F32, name="rstd", tag="rstd")
+            nc.gpsimd.tensor_tensor(out=r[:], in0=var[:], in1=neg_half[:], op=ALU.pow)
+            rstd[i] = r
+
+        def norm(i, u):
+            if u == 0:
+                hsort[i] = actp.tile([P, H], BF16, name="hsort", tag="hsort")
+            gain = ln2b[0 if i < TILES0 else 1]
+            nc.vector.scalar_tensor_tensor(
+                out=hsort[i][:, u * (H // 2) : (u + 1) * (H // 2)].rearrange("p (q e) -> p q e", e=2),
+                in0=xm[i][:].rearrange("p (q u e) -> p u q e", u=2, e=2)[:, u],
+                scalar=rstd[i][:, 0:1],
+                in1=gain[:].rearrange("p (q u e) -> p u q e", u=2, e=2)[:, u],
+                op0=ALU.mult,
+                op1=ALU.mult,
+            )
+
+        def h_transposes(i):
+            words = hsort[i][:].bitcast(F32)
+            gat[i] = transposes(lambda kp, u: words[:, u * NB + kp * P : u * NB + (kp + 1) * P])
+
+        def h_quant(i):
+            for kp in range(KP):
+                nc.vector.quantize_mx(
+                    out=hc[:, i, kp, :].bitcast(FP8X4),
+                    scales=hs[4 * kp :, i, :],
+                    in_=gat[i][:, kp * K_PASS : (kp + 1) * K_PASS],
+                )
+
+        def tile_ok(i):
+            return st["lo"] <= i < st["hi"]
+
+        def block_a(it):
+            if tile_ok(it):
+                s1_matmul(it, 0)
+                s1_matmul(it, 1)
+            if tile_ok(it - 3):
+                h_quant(it - 3)
+            if tile_ok(it - 4):
+                h_ready.add(it - 4)
+
+        def block_b(it):
+            if tile_ok(it + 1):
+                attn_transposes(it + 1)
+            if tile_ok(it):
+                square(it, 0)
+            if tile_ok(it - 1):
+                norm(it - 1, 0)
+            if tile_ok(it + 1):
+                attn_quant(it + 1)
+
+        def block_c(it):
+            if tile_ok(it):
+                s1_matmul(it, 2)
+            if tile_ok(it - 1):
+                norm(it - 1, 1)
+            if tile_ok(it):
+                s1_matmul(it, 3)
+                nc.sync.dma_start(out=out_0[it * P : (it + 1) * P, :], in_=xm[it][:])
+                load_x(it + 2)
+            if it == 0:
+                for g in range(2):
+                    nc.sync.dma_start(out=ln2b[g][:], in_=ln2[g].partition_broadcast(P))
+
+        def block_d(it):
+            if tile_ok(it - 2):
+                h_transposes(it - 2)
+            if tile_ok(it):
+                square(it, 1)
+                inv_rms(it)
+
+        def block_s(c, i, j):
+            wc, ws = codes[j]
+            banks = [accp.tile([P, NB], F32, name="acc", tag="acc") for half in range(2)]
+            for kp in range(KP):
+                for half in range(2):
+                    nc.tensor.matmul_mx(
+                        out=banks[half][:],
+                        lhsT=hc[:, i, kp, :].bitcast(FP8X4),
+                        lhsT_scale=hs[4 * kp :, i, :],
+                        rhs=wc[:, kp, half * NB : (half + 1) * NB].bitcast(FP8X4),
+                        rhs_scale=ws[4 * kp :, half * NB : (half + 1) * NB],
+                        start=(kp == 0),
+                        stop=(kp == KP - 1),
+                    )
+            sg = epi.tile([P, NB], F32, name="sg", tag="sg")
+            nc.scalar.activation(out=sg[:], in_=banks[0][:], func=ACT.Silu)
+            res = epi.tile([P, NB], F32, name="res", tag="res")
+            nc.vector.tensor_tensor(out=res[:], in0=banks[1][:], in1=sg[:], op=ALU.mult)
+            nc.sync.dma_start(out=out_1[i * P : (i + 1) * P, c * NB : (c + 1) * NB], in_=res[:])
+
+        if MANUAL:
+            ctx.enter_context(tc.manual_schedule())
+
+        def ripe(j):
+            return st["quant"] >= UNITS * (j + 1)
+
+        def ripe_step():
+            for j in sorted(steps):
+                if not finished[j] and ripe(j) and steps[j][0][1] in h_ready:
+                    return j
+            return None
+
+        def do_step(j):
+            c, i = steps[j].pop(0)
+            block_s(c, i, j)
+            if not steps[j]:
+                finished[j] = True
+            tick(False)
+
+        load_attn(0)
+        for t in range(RAW_BUFS):
+            unit_load()
+
+        def head_loads():
+            if st["load"] >= UNITS and 1 not in araw:
+                load_x(0)
+                load_attn(1)
+            if st["load"] >= 2 * UNITS and 2 not in araw:
+                load_x(1)
+                load_attn(2)
+
+        blocks = {"a": block_a, "b": block_b, "c": block_c, "d": block_d}
+        for g in range(2):
+            lo, hi = (0, TILES0) if g == 0 else (TILES0, TILES)
+            st["lo"], st["hi"] = lo, hi
+            if g == 1:
+                load_attn(lo)
+                load_attn(lo + 1)
+                load_x(lo)
+                load_x(lo + 1)
+            while g == 1 and not ripe(wo_job[(g, 1)]):
+                j = ripe_step()
+                if j is None:
+                    tick(False)
+                else:
+                    do_step(j)
+            order = [(kind, it) for it in range(lo - 1, hi + 5) for kind in "abcd"]
+            for kind, it in order:
+                if True:
+                    if kind in "ac" and tile_ok(it):
+                        while not ripe(wo_job[(g, 0 if kind == "a" else 1)]):
+                            tick(UNITS * (wo_job[(g, 0 if kind == "a" else 1)] + 1))
+                            head_loads()
+                    blocks[kind](it)
+                    if it == hi - 1 and kind in "ac":
+                        finished[wo_job[(g, 0 if kind == "a" else 1)]] = True
+                    st["who"] = lambda t: t % S1_VEC == 0
+                    for r in range(S1_TICKS[g][kind]):
+                        tick(False)
+                    st["who"] = lambda t: t % 2 == 0
+                    for r in range(S1_STEPS[g][kind] if it < hi else DRAIN_STEPS):
+                        j = ripe_step()
+                        if j is not None:
+                            do_step(j)
+        while True:
+            j = ripe_step()
+            if j is not None:
+                do_step(j)
+            elif st["quant"] < n_units:
+                tick(False)
+            else:
+                break
+        assert all(finished)

@@ -31,8 +31,11 @@ QUANT_LAG = 2
 MANUAL = True
 DRAIN_STEPS = 1
 S1_VEC = 2
-S1_TICKS = ({"a":0,"b":0,"c":0,"d":1}, {"a": 0, "b": 0, "c": 0, "d": 0})
-S1_STEPS = ({"a": 0, "b": 0, "c": 0, "d": 2}, {"a": 1, "b": 1, "c": 1, "d": 1})
+S1_EVERY = 2
+EXTRA_EVERY = 8
+S1_FAST = 8
+S1_TICKS = ({"m": 0, "t": 1}, {"m": 0, "t": 0})
+S1_STEPS = ({"m": 0, "t": 0}, {"m": 2, "t": 2})
 
 
 def tile_twomodelblockrouted_pb_l_kernel(tc, attn, x, W_o, W_gu, ln2, out_0, out_1):
@@ -45,8 +48,8 @@ def tile_twomodelblockrouted_pb_l_kernel(tc, attn, x, W_o, W_gu, ln2, out_0, out
         actp = ctx.enter_context(tc.tile_pool(name="actp", bufs=2))
         smallp = ctx.enter_context(tc.tile_pool(name="smallp", bufs=3))
         epi = ctx.enter_context(tc.tile_pool(name="epi", bufs=4))
-        accp = ctx.enter_context(tc.psum_pool(name="accp", bufs=6))
-        trp = ctx.enter_context(tc.psum_pool(name="trp", bufs=2))
+        accp = ctx.enter_context(tc.psum_pool(name="accp", bufs=4))
+        trp = ctx.enter_context(tc.psum_pool(name="trp", bufs=4))
 
         ident = const.tile([P, P], F32, name="ident", tag="ident")
         make_identity(nc, ident[:])
@@ -56,6 +59,8 @@ def tile_twomodelblockrouted_pb_l_kernel(tc, attn, x, W_o, W_gu, ln2, out_0, out
         nc.gpsimd.memset(warm[:], 0.0)
         warm2 = const.tile([P, 1], F32, name="warm2", tag="warm2")
         nc.scalar.activation(out=warm2[:], in_=warm[:], func=ACT.Silu)
+        ones = const.tile([P, P], BF16, name="ones", tag="ones")
+        nc.vector.memset(ones[:], 1.0)
         junk = const.tile([P, H // 2], BF16, name="junk", tag="junk")
         ln2b = [const.tile([P, H], BF16, name="ln2b%d" % g, tag="ln2b%d" % g) for g in range(2)]
         hc = const.tile([P, TILES, KP, P], U32, name="hc", tag="hc", align_bytes=64)
@@ -79,7 +84,7 @@ def tile_twomodelblockrouted_pb_l_kernel(tc, attn, x, W_o, W_gu, ln2, out_0, out
                 steps[j] = [(c, i) for i in (range(TILES0) if g == 0 else range(TILES0, TILES))]
         finished = [False for jb in jobs]
 
-        st = {"copy": 0, "quant": 0, "load": 0, "lo": 0, "hi": TILES0}
+        st = {"copy": 0, "quant": 0, "load": 0, "lo": 0, "hi": TILES0, "pair": 0}
         h_ready = set()
         st["who"] = lambda t: t % 2 == 0
         raws, grps, codes = {}, {}, {}
@@ -103,8 +108,8 @@ def tile_twomodelblockrouted_pb_l_kernel(tc, attn, x, W_o, W_gu, ln2, out_0, out
         def unit_copy():
             t = st["copy"]
             grp = grpp.tile([P, 4 * NB], BF16, name="grp", tag="grp", align_bytes=64)
-            dst = grp[:].rearrange("p (w j) -> p w j", j=4)
-            src = raws[t][:].rearrange("p j w -> p w j")
+            dst = grp[:].rearrange("p (c i j) -> p c j i", i=4, j=4)
+            src = raws[t][:].rearrange("p j (c i) -> p c j i", i=4)
             if st["who"](t):
                 nc.vector.tensor_copy(out=dst, in_=src)
             else:
@@ -145,6 +150,9 @@ def tile_twomodelblockrouted_pb_l_kernel(tc, attn, x, W_o, W_gu, ln2, out_0, out
             if st["quant"] < st["copy"] - lag:
                 unit_quant()
 
+        def ripe(j):
+            return st["quant"] >= UNITS * (j + 1)
+
         def load_attn(i):
             if i < st["hi"]:
                 t = actp.tile([P, H], BF16, name="araw", tag="araw")
@@ -174,7 +182,7 @@ def tile_twomodelblockrouted_pb_l_kernel(tc, attn, x, W_o, W_gu, ln2, out_0, out
         def attn_transposes(i):
             words = araw[i][:].bitcast(F32)
             gat[i] = transposes(lambda kp, u: words[:, 256 * kp + u : 256 * (kp + 1) : 2])
-            if i > 0:
+            if i > 1:
                 load_attn(i + 2)
 
         def attn_quant(i):
@@ -184,7 +192,11 @@ def tile_twomodelblockrouted_pb_l_kernel(tc, attn, x, W_o, W_gu, ln2, out_0, out
             acod[i] = (c, s)
 
         def s1_matmul(i, n):
-            wc, ws = codes[wo_job[(0 if i < TILES0 else 1, n // 2)]]
+            jb = wo_job[(0 if i < TILES0 else 1, n // 2)]
+            while not ripe(jb):
+                tick(UNITS * (jb + 1))
+                head_loads()
+            wc, ws = codes[jb]
             c, s = acod[i]
             lo = (n % 2) * NB
             o = accp.tile([P, NB], F32, name="acc", tag="acc")
@@ -248,51 +260,65 @@ def tile_twomodelblockrouted_pb_l_kernel(tc, attn, x, W_o, W_gu, ln2, out_0, out
                     in_=gat[i][:, kp * K_PASS : (kp + 1) * K_PASS],
                 )
 
+        gain_rows = []
+
+        def load_gains(g):
+            row = actp.tile([P, H], BF16, name="hsort", tag="hsort")
+            nc.vector.memset(row[:], 0.0)
+            nc.scalar.dma_start(out=row[0:1, :], in_=ln2[g : g + 1, :])
+            gain_rows.append(row)
+
+        def spread_gains(g):
+            row = gain_rows[g]
+            for b in range(2):
+                ps = accp.tile([P, 2 * NB], BF16, name="acc", tag="acc")
+                for a in range(2):
+                    lo = (2 * b + a) * NB
+                    nc.tensor.matmul(out=ps[:, a * NB : (a + 1) * NB], lhsT=ones[:], rhs=row[:, lo : lo + NB], start=True, stop=True)
+                if b == 0:
+                    nc.vector.tensor_copy(out=ln2b[g][:, 2 * b * NB : 2 * (b + 1) * NB], in_=ps[:])
+                else:
+                    nc.scalar.copy(out=ln2b[g][:, 2 * b * NB : 2 * (b + 1) * NB], in_=ps[:])
+
         def tile_ok(i):
             return st["lo"] <= i < st["hi"]
 
-        def block_a(it):
+        def block_m(it):
             if tile_ok(it):
                 s1_matmul(it, 0)
+            if tile_ok(it + 1):
+                attn_quant(it + 1)
+            if tile_ok(it):
                 s1_matmul(it, 1)
+                square(it, 0)
             if tile_ok(it - 3):
                 h_quant(it - 3)
             if tile_ok(it - 4):
                 h_ready.add(it - 4)
-
-        def block_b(it):
-            if tile_ok(it + 1):
-                attn_transposes(it + 1)
-            if tile_ok(it):
-                square(it, 0)
-            if tile_ok(it - 1):
-                norm(it - 1, 0)
-            if tile_ok(it + 1):
-                attn_quant(it + 1)
-
-        def block_c(it):
             if tile_ok(it):
                 s1_matmul(it, 2)
-            if tile_ok(it - 1):
-                norm(it - 1, 1)
-            if tile_ok(it):
                 s1_matmul(it, 3)
                 nc.sync.dma_start(out=out_0[it * P : (it + 1) * P, :], in_=xm[it][:])
                 load_x(it + 2)
-            if it == 0:
-                for g in range(2):
-                    nc.sync.dma_start(out=ln2b[g][:], in_=ln2[g].partition_broadcast(P))
-
-        def block_d(it):
-            if tile_ok(it - 2):
-                h_transposes(it - 2)
-            if tile_ok(it):
                 square(it, 1)
                 inv_rms(it)
+            if tile_ok(it - 1):
+                norm(it - 1, 0)
+                norm(it - 1, 1)
+
+        def block_t(it):
+            if tile_ok(it + 2):
+                attn_transposes(it + 2)
+            if tile_ok(it - 2):
+                h_transposes(it - 2)
 
         def block_s(c, i, j):
             wc, ws = codes[j]
-            banks = [accp.tile([P, NB], F32, name="acc", tag="acc") for half in range(2)]
+            st["pair"] += 1
+            if st["pair"] % 2 == 0:
+                banks = [accp.tile([P, NB], F32, name="acc", tag="acc") for half in range(2)]
+            else:
+                banks = [trp.tile([P, NB], F32, name="tr", tag="tr") for half in range(2)]
             for kp in range(KP):
                 for half in range(2):
                     nc.tensor.matmul_mx(
@@ -313,9 +339,6 @@ def tile_twomodelblockrouted_pb_l_kernel(tc, attn, x, W_o, W_gu, ln2, out_0, out
         if MANUAL:
             ctx.enter_context(tc.manual_schedule())
 
-        def ripe(j):
-            return st["quant"] >= UNITS * (j + 1)
-
         def ripe_step():
             for j in sorted(steps):
                 if not finished[j] and ripe(j) and steps[j][0][1] in h_ready:
@@ -328,20 +351,25 @@ def tile_twomodelblockrouted_pb_l_kernel(tc, attn, x, W_o, W_gu, ln2, out_0, out
             if not steps[j]:
                 finished[j] = True
             tick(False)
+            if len(steps[j]) % EXTRA_EVERY == 1:
+                tick(False)
 
+        load_gains(0)
+        load_gains(1)
         load_attn(0)
+        load_attn(1)
         for t in range(RAW_BUFS):
             unit_load()
 
         def head_loads():
-            if st["load"] >= UNITS and 1 not in araw:
+            if st["load"] >= UNITS and 0 not in xraw:
                 load_x(0)
-                load_attn(1)
             if st["load"] >= 2 * UNITS and 2 not in araw:
-                load_x(1)
                 load_attn(2)
+                load_x(1)
+                load_attn(3)
 
-        blocks = {"a": block_a, "b": block_b, "c": block_c, "d": block_d}
+        blocks = {"m": block_m, "t": block_t}
         for g in range(2):
             lo, hi = (0, TILES0) if g == 0 else (TILES0, TILES)
             st["lo"], st["hi"] = lo, hi
@@ -356,18 +384,18 @@ def tile_twomodelblockrouted_pb_l_kernel(tc, attn, x, W_o, W_gu, ln2, out_0, out
                     tick(False)
                 else:
                     do_step(j)
-            order = [(kind, it) for it in range(lo - 1, hi + 5) for kind in "abcd"]
+            order = [(kind, it) for it in range(lo - 2, hi + 5) for kind in "mt"]
             for kind, it in order:
                 if True:
-                    if kind in "ac" and tile_ok(it):
-                        while not ripe(wo_job[(g, 0 if kind == "a" else 1)]):
-                            tick(UNITS * (wo_job[(g, 0 if kind == "a" else 1)] + 1))
-                            head_loads()
                     blocks[kind](it)
-                    if it == hi - 1 and kind in "ac":
-                        finished[wo_job[(g, 0 if kind == "a" else 1)]] = True
+                    if (kind, it) == ("t", -1):
+                        spread_gains(0)
+                        spread_gains(1)
+                    if it == hi - 1 and kind == "m":
+                        finished[wo_job[(g, 0)]] = True
+                        finished[wo_job[(g, 1)]] = True
                     st["who"] = lambda t: t % S1_VEC == 0
-                    for r in range(S1_TICKS[g][kind]):
+                    for r in range(S1_TICKS[g][kind] if (it % S1_EVERY == 0 or it >= lo + S1_FAST) else 0):
                         tick(False)
                     st["who"] = lambda t: t % 2 == 0
                     for r in range(S1_STEPS[g][kind] if it < hi else DRAIN_STEPS):

@@ -24,18 +24,21 @@ TILES0 = ROWS0 // P
 CHUNKS = FF // NB
 UNITS = 2 * KP
 
-RAW_BUFS = 6
+RAW_BUFS = 3
+RAW_LATE = 2
 GRP_BUFS = 4
 JOB_BUFS = 4
+JOB_LATE = 2
 QUANT_LAG = 2
-MANUAL = True
+RES_BUFS = 4
+SG_BUFS = 3
 DRAIN_STEPS = 1
-S1_VEC = 2
 S1_EVERY = 2
-EXTRA_EVERY = 8
 S1_FAST = 8
+EXTRA_EVERY = 8
 S1_TICKS = ({"m": 0, "t": 1}, {"m": 0, "t": 0})
 S1_STEPS = ({"m": 0, "t": 0}, {"m": 2, "t": 2})
+EARLY_CHUNKS = 5
 
 
 def tile_twomodelblockrouted_pb_l_kernel(tc, attn, x, W_o, W_gu, ln2, out_0, out_1):
@@ -45,11 +48,11 @@ def tile_twomodelblockrouted_pb_l_kernel(tc, attn, x, W_o, W_gu, ln2, out_0, out
         rawp = ctx.enter_context(tc.tile_pool(name="rawp", bufs=RAW_BUFS))
         grpp = ctx.enter_context(tc.tile_pool(name="grpp", bufs=GRP_BUFS))
         wpool = ctx.enter_context(tc.tile_pool(name="wpool", bufs=JOB_BUFS))
-        actp = ctx.enter_context(tc.tile_pool(name="actp", bufs=2))
         smallp = ctx.enter_context(tc.tile_pool(name="smallp", bufs=3))
-        epi = ctx.enter_context(tc.tile_pool(name="epi", bufs=4))
+        epi = ctx.enter_context(tc.tile_pool(name="epi", bufs=3))
         accp = ctx.enter_context(tc.psum_pool(name="accp", bufs=4))
         trp = ctx.enter_context(tc.psum_pool(name="trp", bufs=4))
+        pool = {}
 
         ident = const.tile([P, P], F32, name="ident", tag="ident")
         make_identity(nc, ident[:])
@@ -66,107 +69,166 @@ def tile_twomodelblockrouted_pb_l_kernel(tc, attn, x, W_o, W_gu, ln2, out_0, out
         hc = const.tile([P, TILES, KP, P], U32, name="hc", tag="hc", align_bytes=64)
         hs = const.tile([P, TILES, P], U8, name="hs", tag="hs", align_bytes=64)
 
-        job_list = [("o", 0, 0), ("o", 0, 1), ("g", 0, 0), ("g", 0, 1), ("g", 0, 2), ("g", 0, 3), ("o", 1, 0), ("o", 1, 1), ("g", 0, 4)]
-        c1 = 0
-        for c0 in range(5, CHUNKS):
-            job_list.extend([("g", 1, c1), ("g", 1, c1 + 1), ("g", 0, c0)])
-            c1 += 2
-        jobs = []
-        steps = {}
-        wo_job = {}
-        for j, jb in enumerate(job_list):
-            kind, g, c = jb
-            if kind == "o":
-                jobs.append((W_o[g], (2 * c * NB, (2 * c + 1) * NB)))
-                wo_job[(g, c)] = j
-            else:
-                jobs.append((W_gu[g], (c * NB, FF + c * NB)))
-                steps[j] = [(c, i) for i in (range(TILES0) if g == 0 else range(TILES0, TILES))]
-        finished = [False for jb in jobs]
+        feed, groups, wo_job = [], [], {}
+        st = {"jobs": 0, "copy": 0, "quant": 0, "load": 0, "lo": 0, "hi": TILES0, "pair": 0, "cap": JOB_BUFS, "raw_cap": RAW_BUFS}
 
-        st = {"copy": 0, "quant": 0, "load": 0, "lo": 0, "hi": TILES0, "pair": 0}
-        h_ready = set()
+        def new_job():
+            st["jobs"] += 1
+            return st["jobs"] - 1
+
+        def rows(kp):
+            return slice(kp * K_PASS, (kp + 1) * K_PASS)
+
+        def feed_wo(g):
+            for a in range(2):
+                j = new_job()
+                wo_job[(g, a)] = j
+                for kp in range(KP):
+                    feed.append((True, [W_o[g][rows(kp), 2 * a * NB : 2 * (a + 1) * NB]], [(j, kp, 0), (j, kp, 1)]))
+
+        def feed_chunk(g, c):
+            j = new_job()
+            for kp in range(KP):
+                srcs = [W_gu[g][rows(kp), gu * FF + c * NB : gu * FF + (c + 1) * NB] for gu in range(2)]
+                feed.append((False, srcs, [(j, kp, 0), (j, kp, 1)]))
+            groups.append(([j], c, g))
+
+        def feed_pair(g, c):
+            j0 = new_job()
+            j1 = new_job()
+            for kp in range(KP):
+                for gu in range(2):
+                    src = W_gu[g][rows(kp), gu * FF + c * NB : gu * FF + (c + 2) * NB]
+                    feed.append((True, [src], [(j0, kp, gu), (j1, kp, gu)]))
+            groups.append(([j0, j1], c, g))
+
+        feed_wo(0)
+        for c in range(4):
+            feed_chunk(0, c)
+        feed_wo(1)
+        feed_chunk(0, 4)
+        feed_chunk(0, 5)
+        feed_pair(0, 6)
+        feed_pair(1, 0)
+        feed_pair(1, 2)
+        feed_pair(0, 8)
+        feed_pair(1, 4)
+        feed_pair(1, 6)
+        feed_pair(1, 8)
+
+        n_units = 2 * len(feed)
+        last_unit = {}
+        for t in range(n_units):
+            last_unit[feed[t // 2][2][t % 2][0]] = t
+        todo = [list(range(TILES0) if g == 0 else range(TILES0, TILES)) for jl, c, g in groups]
+        started, finished = set(), set()
+
         st["who"] = lambda t: t % 2 == 0
-        raws, grps, codes = {}, {}, {}
-        araw, xraw, gat, acod, xm, hsort, sums, rstd = {}, {}, {}, {}, {}, {}, {}, {}
-        n_units = UNITS * len(jobs)
+        h_ready = set()
+        raws, grps, codes, where = {}, {}, {}, {}
+        live = {"w": 0, "r": 0}
+        araw, xraw, gat, acod, xm, hsort, sums, rstd, obank = {}, {}, {}, {}, {}, {}, {}, {}, {}
 
-        def unit_load():
-            t = st["load"]
-            if t >= n_units:
-                return
-            w, cols = jobs[t // UNITS]
-            kp, hf = (t % UNITS) // 2, t % 2
-            raw = rawp.tile([P, 4, NB], BF16, name="raw", tag="raw")
-            nc.sync.dma_start(
-                out=raw[:],
-                in_=w[kp * K_PASS : (kp + 1) * K_PASS, cols[hf] : cols[hf] + NB].rearrange("(p j) w -> p j w", j=4),
-            )
-            raws[t] = raw
-            st["load"] = t + 1
+        def fill_raw():
+            while st["load"] < len(feed) and st["load"] - st["copy"] // 2 < st["raw_cap"]:
+                r = st["load"]
+                wide, srcs, halves = feed[r]
+                early = live["r"] < RAW_BUFS
+                src_pool = rawp if early else pool["late"]
+                live["r"] += 1 if early else 0
+                where[("r", r)] = early
+                if wide:
+                    raw = src_pool.tile([P, 4, 2 * NB], BF16, name="raw", tag="raw")
+                    nc.sync.dma_start(out=raw[:], in_=srcs[0].rearrange("(p j) w -> p j w", j=4))
+                    raws[r] = [raw[:, :, hf * NB : (hf + 1) * NB] for hf in range(2)]
+                else:
+                    raw = src_pool.tile([P, 2, 4, NB], BF16, name="raw", tag="raw")
+                    for hf in range(2):
+                        nc.sync.dma_start(out=raw[:, hf], in_=srcs[hf].rearrange("(p j) w -> p j w", j=4))
+                    raws[r] = [raw[:, hf] for hf in range(2)]
+                st["load"] = r + 1
+
+        def can_copy(t):
+            j = feed[t // 2][2][t % 2][0]
+            return j in started or len(started) - len(finished) < st["cap"]
 
         def unit_copy():
             t = st["copy"]
+            started.add(feed[t // 2][2][t % 2][0])
             grp = grpp.tile([P, 4 * NB], BF16, name="grp", tag="grp", align_bytes=64)
             dst = grp[:].rearrange("p (c i j) -> p c j i", i=4, j=4)
-            src = raws[t][:].rearrange("p j (c i) -> p c j i", i=4)
+            src = raws[t // 2][t % 2].rearrange("p j (c i) -> p c j i", i=4)
             if st["who"](t):
                 nc.vector.tensor_copy(out=dst, in_=src)
             else:
                 nc.scalar.copy(out=dst, in_=src)
             grps[t] = grp
             st["copy"] = t + 1
+            if t % 2 == 1 and where[("r", t // 2)]:
+                live["r"] -= 1
 
         def unit_quant():
             t = st["quant"]
-            j = t // UNITS
-            kp, hf = (t % UNITS) // 2, t % 2
-            if t % UNITS == 0:
-                wc = wpool.tile([P, KP, 2 * NB], U32, name="wc", tag="wc", align_bytes=64)
-                ws = wpool.tile([P, 2 * NB], U8, name="ws", tag="ws", align_bytes=64)
+            j, kp, slot = feed[t // 2][2][t % 2]
+            if j not in codes:
+                early = live["w"] < JOB_BUFS
+                src_pool = wpool if early else pool["late"]
+                live["w"] += 1 if early else 0
+                where[("w", j)] = early
+                wc = src_pool.tile([P, KP, 2 * NB], U32, name="wc", tag="wc", align_bytes=64)
+                ws = src_pool.tile([P, 2 * NB], U8, name="ws", tag="ws", align_bytes=64)
                 codes[j] = (wc, ws)
             wc, ws = codes[j]
             nc.vector.quantize_mx(
-                out=wc[:, kp, hf * NB : (hf + 1) * NB].bitcast(FP8X4),
-                scales=ws[4 * kp :, hf * NB : (hf + 1) * NB],
+                out=wc[:, kp, slot * NB : (slot + 1) * NB].bitcast(FP8X4),
+                scales=ws[4 * kp :, slot * NB : (slot + 1) * NB],
                 in_=grps[t][:],
             )
             st["quant"] = t + 1
 
-        def job_free(j):
-            return sum(1 for k in range(j) if not finished[k]) < JOB_BUFS
+        def finish(j):
+            finished.add(j)
+            if where[("w", j)]:
+                live["w"] -= 1
 
-        def tick(flush):
+        def tick(need=0):
             t = st["copy"]
-            copied = False
-            if flush and t >= flush:
+            if need and t >= need:
                 unit_quant()
                 return
-            if t < n_units and job_free(t // UNITS):
+            copied = False
+            if t < n_units and can_copy(t):
                 unit_copy()
-                unit_load()
+                fill_raw()
                 copied = True
-            lag = QUANT_LAG if copied else 0
-            if st["quant"] < st["copy"] - lag:
+            if st["quant"] < st["copy"] - (QUANT_LAG if copied else 0):
                 unit_quant()
 
         def ripe(j):
-            return st["quant"] >= UNITS * (j + 1)
+            return st["quant"] > last_unit[j]
 
         def load_attn(i):
             if i < st["hi"]:
-                t = actp.tile([P, H], BF16, name="araw", tag="araw")
+                t = pool["act"].tile([P, H], BF16, name="araw", tag="araw")
                 nc.sync.dma_start(out=t[:], in_=attn[i * P : (i + 1) * P, :])
                 araw[i] = t
 
         def load_x(i):
             if i < st["hi"]:
-                t = actp.tile([P, H], BF16, name="xraw", tag="xraw")
+                t = pool["act"].tile([P, H], BF16, name="xraw", tag="xraw")
                 nc.sync.dma_start(out=t[:], in_=x[i * P : (i + 1) * P, :])
                 xraw[i] = t
 
+        def head_loads():
+            if st["load"] >= KP and 0 not in xraw:
+                load_x(0)
+            if st["load"] >= 2 * KP and 2 not in araw:
+                load_attn(2)
+                load_x(1)
+                load_attn(3)
+
         def transposes(word_slice):
-            g = actp.tile([P, H], BF16, name="gact", tag="gact", align_bytes=64)
+            g = pool["act"].tile([P, H], BF16, name="gact", tag="gact", align_bytes=64)
             gw = g[:].bitcast(F32)
             for b in range(2):
                 tr = trp.tile([P, NB], F32, name="tr", tag="tr")
@@ -186,15 +248,15 @@ def tile_twomodelblockrouted_pb_l_kernel(tc, attn, x, W_o, W_gu, ln2, out_0, out
                 load_attn(i + 2)
 
         def attn_quant(i):
-            c = actp.tile([P, KP, P], U32, name="ac", tag="ac", align_bytes=64)
-            s = actp.tile([P, KP * P], U8, name="asc", tag="asc", align_bytes=64)
+            c = pool["act"].tile([P, KP, P], U32, name="ac", tag="ac", align_bytes=64)
+            s = pool["act"].tile([P, KP * P], U8, name="asc", tag="asc", align_bytes=64)
             nc.vector.quantize_mx(out=c[:].rearrange("p k r -> p (k r)").bitcast(FP8X4), scales=s[:], in_=gat[i][:])
             acod[i] = (c, s)
 
         def s1_matmul(i, n):
             jb = wo_job[(0 if i < TILES0 else 1, n // 2)]
             while not ripe(jb):
-                tick(UNITS * (jb + 1))
+                tick(last_unit[jb] + 1)
                 head_loads()
             wc, ws = codes[jb]
             c, s = acod[i]
@@ -211,7 +273,7 @@ def tile_twomodelblockrouted_pb_l_kernel(tc, attn, x, W_o, W_gu, ln2, out_0, out
                     stop=(kp == KP - 1),
                 )
             if n == 0:
-                xm[i] = actp.tile([P, H], F32, name="xm", tag="xm")
+                xm[i] = pool["act"].tile([P, H], F32, name="xm", tag="xm")
             nc.vector.tensor_tensor(
                 out=xm[i][:, n * NB : (n + 1) * NB], in0=o[:], in1=xraw[i][:, n * NB : (n + 1) * NB], op=ALU.add
             )
@@ -237,7 +299,7 @@ def tile_twomodelblockrouted_pb_l_kernel(tc, attn, x, W_o, W_gu, ln2, out_0, out
 
         def norm(i, u):
             if u == 0:
-                hsort[i] = actp.tile([P, H], BF16, name="hsort", tag="hsort")
+                hsort[i] = pool["act"].tile([P, H], BF16, name="hsort", tag="hsort")
             gain = ln2b[0 if i < TILES0 else 1]
             nc.vector.scalar_tensor_tensor(
                 out=hsort[i][:, u * (H // 2) : (u + 1) * (H // 2)].rearrange("p (q e) -> p q e", e=2),
@@ -263,7 +325,7 @@ def tile_twomodelblockrouted_pb_l_kernel(tc, attn, x, W_o, W_gu, ln2, out_0, out
         gain_rows = []
 
         def load_gains(g):
-            row = actp.tile([P, H], BF16, name="hsort", tag="hsort")
+            row = pool["act"].tile([P, H], BF16, name="hsort", tag="hsort")
             nc.vector.memset(row[:], 0.0)
             nc.scalar.dma_start(out=row[0:1, :], in_=ln2[g : g + 1, :])
             gain_rows.append(row)
@@ -312,102 +374,97 @@ def tile_twomodelblockrouted_pb_l_kernel(tc, attn, x, W_o, W_gu, ln2, out_0, out
             if tile_ok(it - 2):
                 h_transposes(it - 2)
 
-        def block_s(c, i, j):
-            wc, ws = codes[j]
-            st["pair"] += 1
-            if st["pair"] % 2 == 0:
-                banks = [accp.tile([P, NB], F32, name="acc", tag="acc") for half in range(2)]
-            else:
-                banks = [trp.tile([P, NB], F32, name="tr", tag="tr") for half in range(2)]
-            for kp in range(KP):
-                for half in range(2):
-                    nc.tensor.matmul_mx(
-                        out=banks[half][:],
-                        lhsT=hc[:, i, kp, :].bitcast(FP8X4),
-                        lhsT_scale=hs[4 * kp :, i, :],
-                        rhs=wc[:, kp, half * NB : (half + 1) * NB].bitcast(FP8X4),
-                        rhs_scale=ws[4 * kp :, half * NB : (half + 1) * NB],
-                        start=(kp == 0),
-                        stop=(kp == KP - 1),
-                    )
-            sg = epi.tile([P, NB], F32, name="sg", tag="sg")
-            nc.scalar.activation(out=sg[:], in_=banks[0][:], func=ACT.Silu)
-            res = epi.tile([P, NB], F32, name="res", tag="res")
-            nc.vector.tensor_tensor(out=res[:], in0=banks[1][:], in1=sg[:], op=ALU.mult)
-            nc.sync.dma_start(out=out_1[i * P : (i + 1) * P, c * NB : (c + 1) * NB], in_=res[:])
-
-        if MANUAL:
-            ctx.enter_context(tc.manual_schedule())
-
-        def ripe_step():
-            for j in sorted(steps):
-                if not finished[j] and ripe(j) and steps[j][0][1] in h_ready:
-                    return j
+        def ripe_group():
+            for k in range(len(groups)):
+                if todo[k] and all(ripe(j) for j in groups[k][0]) and todo[k][0] in h_ready:
+                    return k
             return None
 
-        def do_step(j):
-            c, i = steps[j].pop(0)
-            block_s(c, i, j)
-            if not steps[j]:
-                finished[j] = True
-            tick(False)
-            if len(steps[j]) % EXTRA_EVERY == 1:
-                tick(False)
-
-        load_gains(0)
-        load_gains(1)
-        load_attn(0)
-        load_attn(1)
-        for t in range(RAW_BUFS):
-            unit_load()
-
-        def head_loads():
-            if st["load"] >= UNITS and 0 not in xraw:
-                load_x(0)
-            if st["load"] >= 2 * UNITS and 2 not in araw:
-                load_attn(2)
-                load_x(1)
-                load_attn(3)
-
-        blocks = {"m": block_m, "t": block_t}
-        for g in range(2):
-            lo, hi = (0, TILES0) if g == 0 else (TILES0, TILES)
-            st["lo"], st["hi"] = lo, hi
-            if g == 1:
-                load_attn(lo)
-                load_attn(lo + 1)
-                load_x(lo)
-                load_x(lo + 1)
-            while g == 1 and not ripe(wo_job[(g, 1)]):
-                j = ripe_step()
-                if j is None:
-                    tick(False)
+        def do_step(k):
+            jl, c, g = groups[k]
+            i = todo[k].pop(0)
+            res = epi.tile([P, len(jl) * NB], F32, name="res", tag="res", bufs=RES_BUFS)
+            for h, j in enumerate(jl):
+                wc, ws = codes[j]
+                st["pair"] += 1
+                if st["pair"] % 2 == 0:
+                    banks = [accp.tile([P, NB], F32, name="acc", tag="acc") for half in range(2)]
                 else:
-                    do_step(j)
-            order = [(kind, it) for it in range(lo - 2, hi + 5) for kind in "mt"]
-            for kind, it in order:
-                if True:
-                    blocks[kind](it)
-                    if (kind, it) == ("t", -1):
-                        spread_gains(0)
-                        spread_gains(1)
-                    if it == hi - 1 and kind == "m":
-                        finished[wo_job[(g, 0)]] = True
-                        finished[wo_job[(g, 1)]] = True
-                    st["who"] = lambda t: t % S1_VEC == 0
-                    for r in range(S1_TICKS[g][kind] if (it % S1_EVERY == 0 or it >= lo + S1_FAST) else 0):
-                        tick(False)
-                    st["who"] = lambda t: t % 2 == 0
-                    for r in range(S1_STEPS[g][kind] if it < hi else DRAIN_STEPS):
-                        j = ripe_step()
-                        if j is not None:
-                            do_step(j)
-        while True:
-            j = ripe_step()
-            if j is not None:
-                do_step(j)
-            elif st["quant"] < n_units:
-                tick(False)
-            else:
-                break
-        assert all(finished)
+                    banks = [trp.tile([P, NB], F32, name="tr", tag="tr") for half in range(2)]
+                for kp in range(KP):
+                    for half in range(2):
+                        nc.tensor.matmul_mx(
+                            out=banks[half][:],
+                            lhsT=hc[:, i, kp, :].bitcast(FP8X4),
+                            lhsT_scale=hs[4 * kp :, i, :],
+                            rhs=wc[:, kp, half * NB : (half + 1) * NB].bitcast(FP8X4),
+                            rhs_scale=ws[4 * kp :, half * NB : (half + 1) * NB],
+                            start=(kp == 0),
+                            stop=(kp == KP - 1),
+                        )
+                sg = epi.tile([P, NB], F32, name="sg", tag="sg", bufs=SG_BUFS)
+                nc.scalar.activation(out=sg[:], in_=banks[0][:], func=ACT.Silu)
+                nc.vector.tensor_tensor(out=res[:, h * NB : (h + 1) * NB], in0=banks[1][:], in1=sg[:], op=ALU.mult)
+                if h == len(jl) - 1:
+                    nc.sync.dma_start(out=out_1[i * P : (i + 1) * P, c * NB : (c + len(jl)) * NB], in_=res[:])
+                    if not todo[k]:
+                        for jj in jl:
+                            finish(jj)
+                tick()
+            if len(todo[k]) % EXTRA_EVERY == 1:
+                tick()
+
+        ctx.enter_context(tc.manual_schedule())
+
+        with tc.tile_pool(name="actp", bufs=2) as actp:
+            pool["act"] = actp
+            load_gains(0)
+            load_gains(1)
+            load_attn(0)
+            load_attn(1)
+            fill_raw()
+            blocks = {"m": block_m, "t": block_t}
+            for g in range(2):
+                lo, hi = (0, TILES0) if g == 0 else (TILES0, TILES)
+                st["lo"], st["hi"] = lo, hi
+                if g == 1:
+                    load_attn(lo)
+                    load_attn(lo + 1)
+                    load_x(lo)
+                    load_x(lo + 1)
+                while g == 1 and not ripe(wo_job[(g, 1)]):
+                    k = ripe_group()
+                    if k is None:
+                        tick()
+                    else:
+                        do_step(k)
+                for it in range(lo - 2, hi + 5):
+                    for kind in "mt":
+                        blocks[kind](it)
+                        if (kind, it) == ("t", 0):
+                            spread_gains(0)
+                            spread_gains(1)
+                        if it == hi - 1 and kind == "m":
+                            finish(wo_job[(g, 0)])
+                            finish(wo_job[(g, 1)])
+                        for r in range(S1_TICKS[g][kind] if it >= lo and (it % S1_EVERY == 0 or it >= lo + S1_FAST) else 0):
+                            tick()
+                        for r in range(S1_STEPS[g][kind] if it < hi else DRAIN_STEPS):
+                            k = ripe_group()
+                            if k is not None:
+                                do_step(k)
+
+        with tc.tile_pool(name="late", bufs=2) as late:
+            pool["late"] = late
+            st["cap"] += JOB_LATE
+            st["raw_cap"] += RAW_LATE
+            fill_raw()
+            while True:
+                k = ripe_group()
+                if k is not None:
+                    do_step(k)
+                elif st["quant"] < n_units:
+                    tick()
+                else:
+                    break
+        assert len(finished) == st["jobs"]

@@ -30,6 +30,7 @@ GRP_BUFS = 4
 JOB_BUFS = 4
 JOB_LATE = 2
 QUANT_LAG = 2
+HEAD_TICKS = 6
 RES_BUFS = 4
 SG_BUFS = 3
 DRAIN_STEPS = 1
@@ -220,9 +221,8 @@ def tile_twomodelblockrouted_pb_l_kernel(tc, attn, x, W_o, W_gu, ln2, out_0, out
                 xraw[i] = t
 
         def head_loads():
-            if st["load"] >= KP and 0 not in xraw:
+            if st["load"] >= 2 * KP and 0 not in xraw:
                 load_x(0)
-            if st["load"] >= 2 * KP and 2 not in araw:
                 load_attn(2)
                 load_x(1)
                 load_attn(3)
@@ -253,7 +253,7 @@ def tile_twomodelblockrouted_pb_l_kernel(tc, attn, x, W_o, W_gu, ln2, out_0, out
             nc.vector.quantize_mx(out=c[:].rearrange("p k r -> p (k r)").bitcast(FP8X4), scales=s[:], in_=gat[i][:])
             acod[i] = (c, s)
 
-        def s1_matmul(i, n):
+        def s1_matmul(i, n, defer=False):
             jb = wo_job[(0 if i < TILES0 else 1, n // 2)]
             while not ripe(jb):
                 tick(last_unit[jb] + 1)
@@ -272,10 +272,15 @@ def tile_twomodelblockrouted_pb_l_kernel(tc, attn, x, W_o, W_gu, ln2, out_0, out
                     start=(kp == 0),
                     stop=(kp == KP - 1),
                 )
+            obank[(i, n)] = o
+            if not defer:
+                s1_add(i, n)
+
+        def s1_add(i, n):
             if n == 0:
                 xm[i] = pool["act"].tile([P, H], F32, name="xm", tag="xm")
             nc.vector.tensor_tensor(
-                out=xm[i][:, n * NB : (n + 1) * NB], in0=o[:], in1=xraw[i][:, n * NB : (n + 1) * NB], op=ALU.add
+                out=xm[i][:, n * NB : (n + 1) * NB], in0=obank[(i, n)][:], in1=xraw[i][:, n * NB : (n + 1) * NB], op=ALU.add
             )
 
         def square(i, half):
@@ -330,17 +335,24 @@ def tile_twomodelblockrouted_pb_l_kernel(tc, attn, x, W_o, W_gu, ln2, out_0, out
             nc.scalar.dma_start(out=row[0:1, :], in_=ln2[g : g + 1, :])
             gain_rows.append(row)
 
+        gain_banks = []
+
         def spread_gains(g):
             row = gain_rows[g]
             for b in range(2):
-                ps = accp.tile([P, 2 * NB], BF16, name="acc", tag="acc")
+                ps = trp.tile([P, 2 * NB], BF16, name="tr", tag="tr")
                 for a in range(2):
                     lo = (2 * b + a) * NB
                     nc.tensor.matmul(out=ps[:, a * NB : (a + 1) * NB], lhsT=ones[:], rhs=row[:, lo : lo + NB], start=True, stop=True)
+                gain_banks.append(ps)
+
+        def keep_gains(g):
+            for b in range(2):
+                dst = ln2b[g][:, 2 * b * NB : 2 * (b + 1) * NB]
                 if b == 0:
-                    nc.vector.tensor_copy(out=ln2b[g][:, 2 * b * NB : 2 * (b + 1) * NB], in_=ps[:])
+                    nc.vector.tensor_copy(out=dst, in_=gain_banks[2 * g + b][:])
                 else:
-                    nc.scalar.copy(out=ln2b[g][:, 2 * b * NB : 2 * (b + 1) * NB], in_=ps[:])
+                    nc.scalar.copy(out=dst, in_=gain_banks[2 * g + b][:])
 
         def tile_ok(i):
             return st["lo"] <= i < st["hi"]
@@ -368,6 +380,20 @@ def tile_twomodelblockrouted_pb_l_kernel(tc, attn, x, W_o, W_gu, ln2, out_0, out
                 norm(it - 1, 0)
                 norm(it - 1, 1)
 
+        def block_m0():
+            for n in range(4):
+                s1_matmul(0, n, True)
+            keep_gains(0)
+            keep_gains(1)
+            attn_quant(1)
+            for n in range(4):
+                s1_add(0, n)
+                if n % 2 == 1:
+                    square(0, n // 2)
+            nc.sync.dma_start(out=out_0[0:P, :], in_=xm[0][:])
+            load_x(2)
+            inv_rms(0)
+
         def block_t(it):
             if tile_ok(it + 2):
                 attn_transposes(it + 2)
@@ -391,8 +417,8 @@ def tile_twomodelblockrouted_pb_l_kernel(tc, attn, x, W_o, W_gu, ln2, out_0, out
                     banks = [accp.tile([P, NB], F32, name="acc", tag="acc") for half in range(2)]
                 else:
                     banks = [trp.tile([P, NB], F32, name="tr", tag="tr") for half in range(2)]
-                for kp in range(KP):
-                    for half in range(2):
+                for half in range(2):
+                    for kp in range(KP):
                         nc.tensor.matmul_mx(
                             out=banks[half][:],
                             lhsT=hc[:, i, kp, :].bitcast(FP8X4),
@@ -418,11 +444,13 @@ def tile_twomodelblockrouted_pb_l_kernel(tc, attn, x, W_o, W_gu, ln2, out_0, out
 
         with tc.tile_pool(name="actp", bufs=2) as actp:
             pool["act"] = actp
+            fill_raw()
             load_gains(0)
             load_gains(1)
             load_attn(0)
             load_attn(1)
-            fill_raw()
+            for r in range(HEAD_TICKS):
+                tick()
             blocks = {"m": block_m, "t": block_t}
             for g in range(2):
                 lo, hi = (0, TILES0) if g == 0 else (TILES0, TILES)
@@ -440,8 +468,11 @@ def tile_twomodelblockrouted_pb_l_kernel(tc, attn, x, W_o, W_gu, ln2, out_0, out
                         do_step(k)
                 for it in range(lo - 2, hi + 5):
                     for kind in "mt":
-                        blocks[kind](it)
-                        if (kind, it) == ("t", 0):
+                        if (kind, it) == ("m", 0):
+                            block_m0()
+                        else:
+                            blocks[kind](it)
+                        if (kind, it) == ("t", -1):
                             spread_gains(0)
                             spread_gains(1)
                         if it == hi - 1 and kind == "m":

@@ -67,8 +67,8 @@ def tile_twomodelblockrouted_pb_l_kernel(tc, attn, x, W_o, W_gu, ln2, out_0, out
         nc.vector.memset(ones[:], 1.0)
         junk = const.tile([P, H // 2], BF16, name="junk", tag="junk")
         ln2b = [const.tile([P, H], BF16, name="ln2b%d" % g, tag="ln2b%d" % g) for g in range(2)]
-        hc = const.tile([P, TILES, KP, P], U32, name="hc", tag="hc", align_bytes=64)
-        hs = const.tile([P, TILES, P], U8, name="hs", tag="hs", align_bytes=64)
+        hc = const.tile([P, TILES, KP, P], U32, name="hc", tag="hc", align_bytes=256)
+        hs = const.tile([P, TILES, P], U8, name="hs", tag="hs", align_bytes=256)
 
         feed, groups, wo_job = [], [], {}
         st = {"jobs": 0, "copy": 0, "quant": 0, "load": 0, "lo": 0, "hi": TILES0, "pair": 0, "cap": JOB_BUFS, "raw_cap": RAW_BUFS}
@@ -156,7 +156,7 @@ def tile_twomodelblockrouted_pb_l_kernel(tc, attn, x, W_o, W_gu, ln2, out_0, out
         def unit_copy():
             t = st["copy"]
             started.add(feed[t // 2][2][t % 2][0])
-            grp = grpp.tile([P, 4 * NB], BF16, name="grp", tag="grp", align_bytes=64)
+            grp = grpp.tile([P, 4 * NB], BF16, name="grp", tag="grp", align_bytes=256)
             dst = grp[:].rearrange("p (c i j) -> p c j i", i=4, j=4)
             src = raws[t // 2][t % 2].rearrange("p j (c i) -> p c j i", i=4)
             if st["who"](t):
@@ -176,8 +176,8 @@ def tile_twomodelblockrouted_pb_l_kernel(tc, attn, x, W_o, W_gu, ln2, out_0, out
                 src_pool = wpool if early else pool["late"]
                 live["w"] += 1 if early else 0
                 where[("w", j)] = early
-                wc = src_pool.tile([P, KP, 2 * NB], U32, name="wc", tag="wc", align_bytes=64)
-                ws = src_pool.tile([P, 2 * NB], U8, name="ws", tag="ws", align_bytes=64)
+                wc = src_pool.tile([P, KP, 2 * NB], U32, name="wc", tag="wc", align_bytes=256)
+                ws = src_pool.tile([P, 2 * NB], U8, name="ws", tag="ws", align_bytes=256)
                 codes[j] = (wc, ws)
             wc, ws = codes[j]
             nc.vector.quantize_mx(
@@ -228,7 +228,7 @@ def tile_twomodelblockrouted_pb_l_kernel(tc, attn, x, W_o, W_gu, ln2, out_0, out
                 load_attn(3)
 
         def transposes(word_slice):
-            g = pool["act"].tile([P, H], BF16, name="gact", tag="gact", align_bytes=64)
+            g = pool["act"].tile([P, H], BF16, name="gact", tag="gact", align_bytes=256)
             gw = g[:].bitcast(F32)
             for b in range(2):
                 tr = trp.tile([P, NB], F32, name="tr", tag="tr")
@@ -248,8 +248,8 @@ def tile_twomodelblockrouted_pb_l_kernel(tc, attn, x, W_o, W_gu, ln2, out_0, out
                 load_attn(i + 2)
 
         def attn_quant(i):
-            c = pool["act"].tile([P, KP, P], U32, name="ac", tag="ac", align_bytes=64)
-            s = pool["act"].tile([P, KP * P], U8, name="asc", tag="asc", align_bytes=64)
+            c = pool["act"].tile([P, KP, P], U32, name="ac", tag="ac", align_bytes=256)
+            s = pool["act"].tile([P, KP * P], U8, name="asc", tag="asc", align_bytes=256)
             nc.vector.quantize_mx(out=c[:].rearrange("p k r -> p (k r)").bitcast(FP8X4), scales=s[:], in_=gat[i][:])
             acod[i] = (c, s)
 

from contextlib import ExitStack

import concourse.mybir as mybir
from concourse.masks import make_identity

F32 = mybir.dt.float32
BF16 = mybir.dt.bfloat16
U32 = mybir.dt.uint32
U8 = mybir.dt.uint8
FP8X4 = mybir.dt.float8_e4m3fn_x4
ACT = mybir.ActivationFunctionType
ALU = mybir.AluOpType

ROWS, ROWS0, H, FF = 2560, 1920, 2048, 5120
EPS = 1.1920929e-07
FLOPS = 2 * ROWS * H * (H + 2 * FF)

P = 128
K_PASS = 4 * P
KP = H // K_PASS
NB = 512
TILES = ROWS // P
TILES0 = ROWS0 // P
CHUNKS = FF // NB
UNITS = 2 * KP

RAW_BUFS = 3
RAW_LATE = 2
GRP_BUFS = 4
JOB_BUFS = 4
JOB_LATE = 2
QUANT_LAG = 2
HEAD_TICKS = 6
RES_BUFS = 4
SG_BUFS = 3
DRAIN_STEPS = 1
S1_EVERY = 2
S1_FAST = 8
EXTRA_EVERY = 8
S1_TICKS = ({"m": 0, "t": 1}, {"m": 0, "t": 0})
S1_STEPS = ({"m": 0, "t": 0}, {"m": 2, "t": 2})
EARLY_CHUNKS = 5


def tile_twomodelblockrouted_pb_l_kernel(tc, attn, x, W_o, W_gu, ln2, out_0, out_1):
    nc = tc.nc
    with ExitStack() as ctx:
        const = ctx.enter_context(tc.tile_pool(name="const", bufs=1))
        rawp = ctx.enter_context(tc.tile_pool(name="rawp", bufs=RAW_BUFS))
        grpp = ctx.enter_context(tc.tile_pool(name="grpp", bufs=GRP_BUFS))
        wpool = ctx.enter_context(tc.tile_pool(name="wpool", bufs=JOB_BUFS))
        smallp = ctx.enter_context(tc.tile_pool(name="smallp", bufs=3))
        epi = ctx.enter_context(tc.tile_pool(name="epi", bufs=3))
        accp = ctx.enter_context(tc.psum_pool(name="accp", bufs=4))
        trp = ctx.enter_context(tc.psum_pool(name="trp", bufs=4))
        pool = {}

        ident = const.tile([P, P], F32, name="ident", tag="ident")
        make_identity(nc, ident[:])
        neg_half = const.tile([P, 1], F32, name="neg_half", tag="neg_half")
        nc.gpsimd.memset(neg_half[:], -0.5)
        warm = const.tile([P, 1], F32, name="warm", tag="warm")
        nc.gpsimd.memset(warm[:], 0.0)
        warm2 = const.tile([P, 1], F32, name="warm2", tag="warm2")
        nc.scalar.activation(out=warm2[:], in_=warm[:], func=ACT.Silu)
        ones = const.tile([P, P], BF16, name="ones", tag="ones")
        nc.vector.memset(ones[:], 1.0)
        junk = const.tile([P, H // 2], BF16, name="junk", tag="junk")
        ln2b = [const.tile([P, H], BF16, name="ln2b%d" % g, tag="ln2b%d" % g) for g in range(2)]
        hc = const.tile([P, TILES, KP, P], U32, name="hc", tag="hc", align_bytes=256)
        hs = const.tile([P, TILES, P], U8, name="hs", tag="hs", align_bytes=256)

        feed, groups, wo_job = [], [], {}
        st = {"jobs": 0, "copy": 0, "quant": 0, "load": 0, "lo": 0, "hi": TILES0, "pair": 0, "cap": JOB_BUFS, "raw_cap": RAW_BUFS}

        def new_job():
            st["jobs"] += 1
            return st["jobs"] - 1

        def rows(kp):
            return slice(kp * K_PASS, (kp + 1) * K_PASS)

        def feed_wo(g):
            for a in range(2):
                j = new_job()
                wo_job[(g, a)] = j
                for kp in range(KP):
                    feed.append((True, [W_o[g][rows(kp), 2 * a * NB : 2 * (a + 1) * NB]], [(j, kp, 0), (j, kp, 1)]))

        def feed_chunk(g, c):
            j = new_job()
            for kp in range(KP):
                srcs = [W_gu[g][rows(kp), gu * FF + c * NB : gu * FF + (c + 1) * NB] for gu in range(2)]
                feed.append((False, srcs, [(j, kp, 0), (j, kp, 1)]))
            groups.append(([j], c, g))

        def feed_pair(g, c):
            j0 = new_job()
            j1 = new_job()
            for kp in range(KP):
                for gu in range(2):
                    src = W_gu[g][rows(kp), gu * FF + c * NB : gu * FF + (c + 2) * NB]
                    feed.append((True, [src], [(j0, kp, gu), (j1, kp, gu)]))
            groups.append(([j0, j1], c, g))

        feed_wo(0)
        for c in range(4):
            feed_chunk(0, c)
        feed_wo(1)
        feed_chunk(0, 4)
        feed_chunk(0, 5)
        feed_pair(0, 6)
        feed_pair(1, 0)
        feed_pair(1, 2)
        feed_pair(0, 8)
        feed_pair(1, 4)
        feed_pair(1, 6)
        feed_pair(1, 8)

        n_units = 2 * len(feed)
        last_unit = {}
        for t in range(n_units):
            last_unit[feed[t // 2][2][t % 2][0]] = t
        todo = [list(range(TILES0) if g == 0 else range(TILES0, TILES)) for jl, c, g in groups]
        started, finished = set(), set()

        st["who"] = lambda t: t % 2 == 0
        h_ready = set()
        raws, grps, codes, where = {}, {}, {}, {}
        live = {"w": 0, "r": 0}
        araw, xraw, gat, acod, xm, hsort, sums, rstd, obank = {}, {}, {}, {}, {}, {}, {}, {}, {}

        def fill_raw():
            while st["load"] < len(feed) and st["load"] - st["copy"] // 2 < st["raw_cap"]:
                r = st["load"]
                wide, srcs, halves = feed[r]
                early = live["r"] < RAW_BUFS
                src_pool = rawp if early else pool["late"]
                live["r"] += 1 if early else 0
                where[("r", r)] = early
                if wide:
                    raw = src_pool.tile([P, 4, 2 * NB], BF16, name="raw", tag="raw")
                    nc.sync.dma_start(out=raw[:], in_=srcs[0].rearrange("(p j) w -> p j w", j=4))
                    raws[r] = [raw[:, :, hf * NB : (hf + 1) * NB] for hf in range(2)]
                else:
                    raw = src_pool.tile([P, 2, 4, NB], BF16, name="raw", tag="raw")
                    for hf in range(2):
                        nc.sync.dma_start(out=raw[:, hf], in_=srcs[hf].rearrange("(p j) w -> p j w", j=4))
                    raws[r] = [raw[:, hf] for hf in range(2)]
                st["load"] = r + 1

        def can_copy(t):
            j = feed[t // 2][2][t % 2][0]
            return j in started or len(started) - len(finished) < st["cap"]

        def unit_copy():
            t = st["copy"]
            started.add(feed[t // 2][2][t % 2][0])
            grp = grpp.tile([P, 4 * NB], BF16, name="grp", tag="grp", align_bytes=256)
            dst = grp[:].rearrange("p (c i j) -> p c j i", i=4, j=4)
            src = raws[t // 2][t % 2].rearrange("p j (c i) -> p c j i", i=4)
            if st["who"](t):
                nc.vector.tensor_copy(out=dst, in_=src)
            else:
                nc.scalar.copy(out=dst, in_=src)
            grps[t] = grp
            st["copy"] = t + 1
            if t % 2 == 1 and where[("r", t // 2)]:
                live["r"] -= 1

        def unit_quant():
            t = st["quant"]
            j, kp, slot = feed[t // 2][2][t % 2]
            if j not in codes:
                early = live["w"] < JOB_BUFS
                src_pool = wpool if early else pool["late"]
                live["w"] += 1 if early else 0
                where[("w", j)] = early
                wc = src_pool.tile([P, KP, 2 * NB], U32, name="wc", tag="wc", align_bytes=256)
                ws = src_pool.tile([P, 2 * NB], U8, name="ws", tag="ws", align_bytes=256)
                codes[j] = (wc, ws)
            wc, ws = codes[j]
            nc.vector.quantize_mx(
                out=wc[:, kp, slot * NB : (slot + 1) * NB].bitcast(FP8X4),
                scales=ws[4 * kp :, slot * NB : (slot + 1) * NB],
                in_=grps[t][:],
            )
            st["quant"] = t + 1

        def finish(j):
            finished.add(j)
            if where[("w", j)]:
                live["w"] -= 1

        def tick(need=0):
            t = st["copy"]
            if need and t >= need:
                unit_quant()
                return
            copied = False
            if t < n_units and can_copy(t):
                unit_copy()
                fill_raw()
                copied = True
            if st["quant"] < st["copy"] - (QUANT_LAG if copied else 0):
                unit_quant()

        def ripe(j):
            return st["quant"] > last_unit[j]

        def load_attn(i):
            if i < st["hi"]:
                t = pool["act"].tile([P, H], BF16, name="araw", tag="araw")
                nc.sync.dma_start(out=t[:], in_=attn[i * P : (i + 1) * P, :])
                araw[i] = t

        def load_x(i):
            if i < st["hi"]:
                t = pool["act"].tile([P, H], BF16, name="xraw", tag="xraw")
                nc.sync.dma_start(out=t[:], in_=x[i * P : (i + 1) * P, :])
                xraw[i] = t

        def head_loads():
            if st["load"] >= 2 * KP and 0 not in xraw:
                load_x(0)
                load_attn(2)
                load_x(1)
                load_attn(3)

        def transposes(word_slice):
            g = pool["act"].tile([P, H], BF16, name="gact", tag="gact", align_bytes=256)
            gw = g[:].bitcast(F32)
            for b in range(2):
                tr = trp.tile([P, NB], F32, name="tr", tag="tr")
                for a in range(2):
                    for u in range(2):
                        nc.tensor.transpose(tr[:, (2 * a + u) * P : (2 * a + u + 1) * P], word_slice(2 * b + a, u), ident[:])
                nc.scalar.copy(
                    out=gw[:, NB * b : NB * (b + 1)].rearrange("p (a r u) -> p a r u", a=2, u=2),
                    in_=tr[:].rearrange("p (a u r) -> p a r u", a=2, u=2),
                )
            return g

        def attn_transposes(i):
            words = araw[i][:].bitcast(F32)
            gat[i] = transposes(lambda kp, u: words[:, 256 * kp + u : 256 * (kp + 1) : 2])
            if i > 1:
                load_attn(i + 2)

        def attn_quant(i):
            c = pool["act"].tile([P, KP, P], U32, name="ac", tag="ac", align_bytes=256)
            s = pool["act"].tile([P, KP * P], U8, name="asc", tag="asc", align_bytes=256)
            nc.vector.quantize_mx(out=c[:].rearrange("p k r -> p (k r)").bitcast(FP8X4), scales=s[:], in_=gat[i][:])
            acod[i] = (c, s)

        def s1_matmul(i, n, defer=False):
            jb = wo_job[(0 if i < TILES0 else 1, n // 2)]
            while not ripe(jb):
                tick(last_unit[jb] + 1)
                head_loads()
            wc, ws = codes[jb]
            c, s = acod[i]
            lo = (n % 2) * NB
            o = accp.tile([P, NB], F32, name="acc", tag="acc")
            for kp in range(KP):
                nc.tensor.matmul_mx(
                    out=o[:],
                    lhsT=c[:, kp, :].bitcast(FP8X4),
                    lhsT_scale=s[:, kp * P : (kp + 1) * P],
                    rhs=wc[:, kp, lo : lo + NB].bitcast(FP8X4),
                    rhs_scale=ws[4 * kp :, lo : lo + NB],
                    start=(kp == 0),
                    stop=(kp == KP - 1),
                )
            obank[(i, n)] = o
            if not defer:
                s1_add(i, n)

        def s1_add(i, n):
            if n == 0:
                xm[i] = pool["act"].tile([P, H], F32, name="xm", tag="xm")
            nc.vector.tensor_tensor(
                out=xm[i][:, n * NB : (n + 1) * NB], in0=obank[(i, n)][:], in1=xraw[i][:, n * NB : (n + 1) * NB], op=ALU.add
            )

        def square(i, half):
            if half == 0:
                sums[i] = smallp.tile([P, 2], F32, name="sums", tag="sums")
            nc.scalar.activation(
                out=junk[:],
                in_=xm[i][:, half * (H // 2) : (half + 1) * (H // 2)],
                func=ACT.Square,
                accum_out=sums[i][:, half : half + 1],
            )

        def inv_rms(i):
            tot = smallp.tile([P, 1], F32, name="tot", tag="tot")
            nc.gpsimd.tensor_tensor(out=tot[:], in0=sums[i][:, 0:1], in1=sums[i][:, 1:2], op=ALU.add)
            var = smallp.tile([P, 1], F32, name="var", tag="var")
            nc.gpsimd.tensor_scalar(out=var[:], in0=tot[:], scalar1=1.0 / H, scalar2=EPS, op0=ALU.mult, op1=ALU.add)
            r = smallp.tile([P, 1], F32, name="rstd", tag="rstd")
            nc.gpsimd.tensor_tensor(out=r[:], in0=var[:], in1=neg_half[:], op=ALU.pow)
            rstd[i] = r

        def norm(i, u):
            if u == 0:
                hsort[i] = pool["act"].tile([P, H], BF16, name="hsort", tag="hsort")
            gain = ln2b[0 if i < TILES0 else 1]
            nc.vector.scalar_tensor_tensor(
                out=hsort[i][:, u * (H // 2) : (u + 1) * (H // 2)].rearrange("p (q e) -> p q e", e=2),
                in0=xm[i][:].rearrange("p (q u e) -> p u q e", u=2, e=2)[:, u],
                scalar=rstd[i][:, 0:1],
                in1=gain[:].rearrange("p (q u e) -> p u q e", u=2, e=2)[:, u],
                op0=ALU.mult,
                op1=ALU.mult,
            )

        def h_transposes(i):
            words = hsort[i][:].bitcast(F32)
            gat[i] = transposes(lambda kp, u: words[:, u * NB + kp * P : u * NB + (kp + 1) * P])

        def h_quant(i):
            for kp in range(KP):
                nc.vector.quantize_mx(
                    out=hc[:, i, kp, :].bitcast(FP8X4),
                    scales=hs[4 * kp :, i, :],
                    in_=gat[i][:, kp * K_PASS : (kp + 1) * K_PASS],
                )

        gain_rows = []

        def load_gains(g):
            row = pool["act"].tile([P, H], BF16, name="hsort", tag="hsort")
            nc.vector.memset(row[:], 0.0)
            nc.scalar.dma_start(out=row[0:1, :], in_=ln2[g : g + 1, :])
            gain_rows.append(row)

        gain_banks = []

        def spread_gains(g):
            row = gain_rows[g]
            for b in range(2):
                ps = trp.tile([P, 2 * NB], BF16, name="tr", tag="tr")
                for a in range(2):
                    lo = (2 * b + a) * NB
                    nc.tensor.matmul(out=ps[:, a * NB : (a + 1) * NB], lhsT=ones[:], rhs=row[:, lo : lo + NB], start=True, stop=True)
                gain_banks.append(ps)

        def keep_gains(g):
            for b in range(2):
                dst = ln2b[g][:, 2 * b * NB : 2 * (b + 1) * NB]
                if b == 0:
                    nc.vector.tensor_copy(out=dst, in_=gain_banks[2 * g + b][:])
                else:
                    nc.scalar.copy(out=dst, in_=gain_banks[2 * g + b][:])

        def tile_ok(i):
            return st["lo"] <= i < st["hi"]

        def block_m(it):
            if tile_ok(it):
                s1_matmul(it, 0)
            if tile_ok(it + 1):
                attn_quant(it + 1)
            if tile_ok(it):
                s1_matmul(it, 1)
                square(it, 0)
            if tile_ok(it - 3):
                h_quant(it - 3)
            if tile_ok(it - 4):
                h_ready.add(it - 4)
            if tile_ok(it):
                s1_matmul(it, 2)
                s1_matmul(it, 3)
                nc.sync.dma_start(out=out_0[it * P : (it + 1) * P, :], in_=xm[it][:])
                load_x(it + 2)
                square(it, 1)
                inv_rms(it)
            if tile_ok(it - 1):
                norm(it - 1, 0)
                norm(it - 1, 1)

        def block_m0():
            for n in range(4):
                s1_matmul(0, n, True)
            keep_gains(0)
            keep_gains(1)
            attn_quant(1)
            for n in range(4):
                s1_add(0, n)
                if n % 2 == 1:
                    square(0, n // 2)
            nc.sync.dma_start(out=out_0[0:P, :], in_=xm[0][:])
            load_x(2)
            inv_rms(0)

        def block_t(it):
            if tile_ok(it + 2):
                attn_transposes(it + 2)
            if tile_ok(it - 2):
                h_transposes(it - 2)

        def ripe_group():
            for k in range(len(groups)):
                if todo[k] and all(ripe(j) for j in groups[k][0]) and todo[k][0] in h_ready:
                    return k
            return None

        def do_step(k):
            jl, c, g = groups[k]
            i = todo[k].pop(0)
            res = epi.tile([P, len(jl) * NB], F32, name="res", tag="res", bufs=RES_BUFS)
            for h, j in enumerate(jl):
                wc, ws = codes[j]
                st["pair"] += 1
                if st["pair"] % 2 == 0:
                    banks = [accp.tile([P, NB], F32, name="acc", tag="acc") for half in range(2)]
                else:
                    banks = [trp.tile([P, NB], F32, name="tr", tag="tr") for half in range(2)]
                for half in range(2):
                    for kp in range(KP):
                        nc.tensor.matmul_mx(
                            out=banks[half][:],
                            lhsT=hc[:, i, kp, :].bitcast(FP8X4),
                            lhsT_scale=hs[4 * kp :, i, :],
                            rhs=wc[:, kp, half * NB : (half + 1) * NB].bitcast(FP8X4),
                            rhs_scale=ws[4 * kp :, half * NB : (half + 1) * NB],
                            start=(kp == 0),
                            stop=(kp == KP - 1),
                        )
                sg = epi.tile([P, NB], F32, name="sg", tag="sg", bufs=SG_BUFS)
                nc.scalar.activation(out=sg[:], in_=banks[0][:], func=ACT.Silu)
                nc.vector.tensor_tensor(out=res[:, h * NB : (h + 1) * NB], in0=banks[1][:], in1=sg[:], op=ALU.mult)
                if h == len(jl) - 1:
                    nc.sync.dma_start(out=out_1[i * P : (i + 1) * P, c * NB : (c + len(jl)) * NB], in_=res[:])
                    if not todo[k]:
                        for jj in jl:
                            finish(jj)
                tick()
            if len(todo[k]) % EXTRA_EVERY == 1:
                tick()

        ctx.enter_context(tc.manual_schedule())

        with tc.tile_pool(name="actp", bufs=2) as actp:
            pool["act"] = actp
            fill_raw()
            load_gains(0)
            load_gains(1)
            load_attn(0)
            load_attn(1)
            for r in range(HEAD_TICKS):
                tick()
            blocks = {"m": block_m, "t": block_t}
            for g in range(2):
                lo, hi = (0, TILES0) if g == 0 else (TILES0, TILES)
                st["lo"], st["hi"] = lo, hi
                if g == 1:
                    load_attn(lo)
                    load_attn(lo + 1)
                    load_x(lo)
                    load_x(lo + 1)
                while g == 1 and not ripe(wo_job[(g, 1)]):
                    k = ripe_group()
                    if k is None:
                        tick()
                    else:
                        do_step(k)
                for it in range(lo - 2, hi + 5):
                    for kind in "mt":
                        if (kind, it) == ("m", 0):
                            block_m0()
                        else:
                            blocks[kind](it)
                        if (kind, it) == ("t", -1):
                            spread_gains(0)
                            spread_gains(1)
                        if it == hi - 1 and kind == "m":
                            finish(wo_job[(g, 0)])
                            finish(wo_job[(g, 1)])
                        for r in range(S1_TICKS[g][kind] if it >= lo and (it % S1_EVERY == 0 or it >= lo + S1_FAST) else 0):
                            tick()
                        for r in range(S1_STEPS[g][kind] if it < hi else DRAIN_STEPS):
                            k = ripe_group()
                            if k is not None:
                                do_step(k)

        with tc.tile_pool(name="late", bufs=2) as late:
            pool["late"] = late
            st["cap"] += JOB_LATE
            st["raw_cap"] += RAW_LATE
            fill_raw()
            while True:
                k = ripe_group()
                if k is not None:
                    do_step(k)
                elif st["quant"] < n_units:
                    tick()
                else:
                    break
        assert len(finished) == st["jobs"]
